import numpy as np
import ml_dtypes


def mxq(x, axis, fmt="e4m3"):
    dtype, down = {"e4m3": (ml_dtypes.float8_e4m3fn, 7), "e5m2": (ml_dtypes.float8_e5m2, 14)}[fmt]
    v = np.moveaxis(np.asarray(x, np.float32).astype(ml_dtypes.bfloat16).astype(np.float64), axis, -1)
    blocks = v.reshape(v.shape[:-1] + (-1, 32))
    amax = np.abs(blocks).max(-1, keepdims=True)
    byte = np.maximum(np.where(amax > 0, np.frexp(amax)[1] - 1 + 127, 0) - down, 1)
    scale = np.exp2(byte - 127.0)
    codes = (blocks / scale).astype(np.float32).astype(dtype).astype(np.float64)
    return np.moveaxis((codes * scale).reshape(v.shape), -1, axis)


WIDE = False


def mx_kscale(k):
    if not WIDE:
        return np.ones(k)
    levels = np.array([10, -10, 5, -5, 0])
    a = np.random.permutation(np.resize(levels, k // 512 * 4)).reshape(k // 512, 4)
    idx = np.arange(k)
    return np.exp2(a[idx // 512, idx % 128 // 32])


BF16 = ml_dtypes.bfloat16


def bf(x):
    return np.asarray(x, np.float32).astype(BF16)


def f64(x):
    return np.asarray(x).astype(np.float64)


B, L, E, H, C, EO = 1, 1024, 2048, 16, 512, 2048
EPS = 1e-8


def sigmoid(v):
    return 1.0 / (1.0 + np.exp(-v))


def setup_inputs():
    s = mx_kscale(E)
    return {"o_attn": bf(np.random.standard_normal((L, B, E)) * 2.0),
            "Wo": bf(np.random.standard_normal((EO, E)) / np.sqrt(E) / s),
            "bo": bf(np.random.standard_normal(EO) * 0.1),
            "norm_scale": bf((1.0 + 0.1 * np.random.standard_normal(E)) * s),
            "norm_gate": bf(1.0 + 0.1 * np.random.standard_normal(E))}


def reference(o_attn, Wo, bo, norm_scale, norm_gate):
    o = f64(o_attn)
    rms = np.sqrt(np.sum(o * o, -1, keepdims=True)) * E ** -0.5
    y = f64(norm_scale) * (o / (rms + EPS)) * sigmoid(f64(norm_gate) * o)
    return (mxq(y, 2, "e4m3") @ mxq(f64(Wo), 1, "e4m3").T) + f64(bo)

@@ -1,0 +1,241 @@
+from contextlib import ExitStack
+
+import concourse.mybir as mybir
+from concourse.masks import make_identity
+
+F32 = mybir.dt.float32
+BF16 = mybir.dt.bfloat16
+U32 = mybir.dt.uint32
+U8 = mybir.dt.uint8
+FP8X4 = mybir.dt.float8_e4m3fn_x4
+ACT = mybir.ActivationFunctionType
+ALU = mybir.AluOpType
+
+P = 128
+L = 1024
+K = 2048
+N = 2048
+EPS = 1e-8
+
+PACK = 4
+K_PASS = P * PACK
+PASSES = K // K_PASS
+PAIR = 2
+HALVES = PACK // PAIR
+BLOCK_K = P * PAIR
+BLOCKS = K // BLOCK_K
+
+L_GROUP = 256
+L_TILES = L_GROUP // P
+GROUPS = L // L_GROUP
+N_CHUNK = 512
+CHUNKS = N // N_CHUNK
+N_LOAD = 256
+N_TILES = N_LOAD // P
+LOADS_PER_CHUNK = N_CHUNK // N_LOAD
+
+FLOPS = 2 * L * K * N
+
+
+def tile_normlocalattention_pb_kernel(tc, o_attn, Wo, bo, norm_scale, norm_gate, out):
+    nc = tc.nc
+    o_rows = o_attn.flatten_outer_dims()
+    out_rows = out.flatten_outer_dims()
+
+    with ExitStack() as stack:
+        keep = stack.enter_context(tc.tile_pool(name="keep", bufs=1))
+        work = stack.enter_context(tc.tile_pool(name="work", bufs=2))
+        results = stack.enter_context(tc.tile_pool(name="results", bufs=4))
+        flipped = stack.enter_context(tc.psum_pool(name="flipped", bufs=5))
+        sums = stack.enter_context(tc.psum_pool(name="sums", bufs=3))
+
+        ident = keep.tile([P, P], F32)
+        make_identity(nc, ident[:])
+        half = keep.tile([P, L_TILES], F32)
+        nc.vector.memset(half[:], 0.5)
+        vec_rows = keep.tile([P, BLOCK_K], BF16)
+        nc.vector.memset(vec_rows[:], 0.0)
+
+        nc.sync.dma_start(out=vec_rows[0:BLOCKS, :], in_=norm_gate.rearrange("(b c) -> b c", c=BLOCK_K))
+        nc.sync.dma_start(
+            out=vec_rows[BLOCKS : 2 * BLOCKS, :], in_=norm_scale.rearrange("(b c) -> b c", c=BLOCK_K)
+        )
+        o_sb = [keep.tile([P, L_TILES, K], BF16, name="o_sb%d" % j) for j in range(GROUPS)]
+        w_sb = [keep.tile([P, N_TILES, K], BF16, name="w_sb%d" % h) for h in range(N // N_LOAD)]
+        bias = keep.tile([P, N], BF16)
+
+        def load_o(j):
+            rows = o_rows[j * L_GROUP : (j + 1) * L_GROUP, :]
+            nc.sync.dma_start(out=o_sb[j][:], in_=rows.rearrange("(i p) k -> p i k", p=P))
+
+        def load_w(c):
+            for h in range(c * LOADS_PER_CHUNK, (c + 1) * LOADS_PER_CHUNK):
+                rows = Wo[h * N_LOAD : (h + 1) * N_LOAD, :]
+                nc.sync.dma_start(out=w_sb[h][:], in_=rows.rearrange("(i p) k -> p i k", p=P))
+
+        load_o(0)
+        load_w(0)
+        load_o(1)
+        nc.sync.dma_start(out=bias[:], in_=bo.partition_broadcast(P))
+        load_w(1)
+        load_o(2)
+        load_o(3)
+        load_w(2)
+        load_w(3)
+
+        vec_t = flipped.tile([P, HALVES, N_LOAD], F32, tag="flip")
+        nc.tensor.transpose(vec_t[:, 0, 0:P], vec_rows[:].bitcast(F32), ident[:])
+        per_channel = keep.tile([P, 2 * BLOCKS * PAIR], F32)
+        nc.vector.tensor_copy(
+            out=per_channel[:], in_=vec_t[:, 0, 0 : 2 * BLOCKS].bitcast(BF16)
+        )
+
+        def gate_of(b, e):
+            col = b * PAIR + e
+            return per_channel[:, col : col + 1]
+
+        def scale_of(b, e):
+            col = (BLOCKS + b) * PAIR + e
+            return per_channel[:, col : col + 1]
+
+        y_codes = keep.tile([P, PASSES, L], U32, align_bytes=64)
+        y_scales = keep.tile([P, PASSES, L], U8, align_bytes=64)
+        w_codes = keep.tile([P, PASSES, N], U32, align_bytes=64)
+        w_scales = keep.tile([P, PASSES, N], U8, align_bytes=64)
+        inv_r = keep.tile([P, L], F32)
+
+        def flip_words(rows_sb, g):
+            bank = flipped.tile([P, HALVES, N_LOAD], F32, tag="flip")
+            for u in range(HALVES):
+                b = g * HALVES + u
+                for i in range(N_TILES):
+                    nc.tensor.transpose(
+                        bank[:, u, i * P : (i + 1) * P],
+                        rows_sb[:, i, :].bitcast(F32)[:, b * P : (b + 1) * P],
+                        ident[:],
+                    )
+            return bank
+
+        def norms(j):
+            sum_sq = work.tile([P, L_TILES], F32)
+            for i in range(L_TILES):
+                squares = work.tile([P, K], BF16)
+                nc.scalar.activation(
+                    out=squares[:], in_=o_sb[j][:, i, :], func=ACT.Square, accum_out=sum_sq[:, i : i + 1]
+                )
+            root = work.tile([P, L_TILES], F32)
+            nc.gpsimd.tensor_tensor(out=root[:], in0=sum_sq[:], in1=half[:], op=ALU.pow)
+            r_eps = work.tile([P, L_TILES], F32)
+            nc.vector.tensor_scalar(
+                out=r_eps[:], in0=root[:], scalar1=K**-0.5, scalar2=EPS, op0=ALU.mult, op1=ALU.add
+            )
+            inv = work.tile([P, L_TILES], F32)
+            nc.vector.reciprocal(out=inv[:], in_=r_eps[:])
+            repeated = work.tile([P, L_TILES, P], F32)
+            nc.vector.tensor_copy(out=repeated[:], in_=inv[:].unsqueeze(2).to_broadcast([P, L_TILES, P]))
+            spread = flipped.tile([P, HALVES, N_LOAD], F32, tag="flip")
+            for i in range(L_TILES):
+                nc.tensor.transpose(spread[:, 0, i * P : (i + 1) * P], repeated[:, i, :], ident[:])
+            nc.vector.tensor_copy(out=inv_r[:, j * L_GROUP : (j + 1) * L_GROUP], in_=spread[:, 0, :])
+
+        def quantise_y(j, g):
+            cols = slice(j * L_GROUP, (j + 1) * L_GROUP)
+            bank = flip_words(o_sb[j], g)
+            o_t = bank[:].bitcast(BF16).rearrange("p u (l e) -> p u l e", e=PAIR)
+            gated = work.tile([P, PACK, L_GROUP], F32)
+            for u in range(HALVES):
+                for e in range(PAIR):
+                    nc.scalar.activation(
+                        out=gated[:, u * PAIR + e, :],
+                        in_=o_t[:, u, :, e],
+                        func=ACT.Sigmoid,
+                        scale=gate_of(g * HALVES + u, e),
+                    )
+            scaled = work.tile([P, PACK, L_GROUP], F32)
+            for u in range(HALVES):
+                for e in range(PAIR):
+                    nc.vector.scalar_tensor_tensor(
+                        out=scaled[:, u * PAIR + e, :],
+                        in0=o_t[:, u, :, e],
+                        scalar=scale_of(g * HALVES + u, e),
+                        in1=gated[:, u * PAIR + e, :],
+                        op0=ALU.mult,
+                        op1=ALU.mult,
+                    )
+            y_bf = work.tile([P, L_GROUP, PACK], BF16, align_bytes=64)
+            nc.vector.tensor_tensor(
+                out=y_bf[:],
+                in0=scaled[:].rearrange("p t l -> p l t"),
+                in1=inv_r[:, cols].unsqueeze(2).to_broadcast([P, L_GROUP, PACK]),
+                op=ALU.mult,
+            )
+            nc.vector.quantize_mx(
+                out=y_codes[:, g, cols].bitcast(FP8X4),
+                scales=y_scales[:, g, cols],
+                in_=y_bf[:].rearrange("p l t -> p (l t)"),
+            )
+
+        def quantise_w(c, g):
+            cols = slice(c * N_CHUNK, (c + 1) * N_CHUNK)
+            w_bf = work.tile([P, N_CHUNK, PACK], BF16, align_bytes=64)
+            for h in range(LOADS_PER_CHUNK):
+                bank = flip_words(w_sb[c * LOADS_PER_CHUNK + h], g)
+                nc.scalar.copy(
+                    out=w_bf[:].bitcast(F32)[:, h * N_LOAD : (h + 1) * N_LOAD, :],
+                    in_=bank[:].rearrange("p u n -> p n u"),
+                )
+            nc.vector.quantize_mx(
+                out=w_codes[:, g, cols].bitcast(FP8X4),
+                scales=w_scales[:, g, cols],
+                in_=w_bf[:].rearrange("p n t -> p (n t)"),
+            )
+
+        def multiply(j, c):
+            n_cols = slice(c * N_CHUNK, (c + 1) * N_CHUNK)
+            for i in range(L_TILES):
+                l_cols = slice(j * L_GROUP + i * P, j * L_GROUP + (i + 1) * P)
+                acc = sums.tile([P, N_CHUNK], F32)
+                for g in range(PASSES):
+                    nc.tensor.matmul_mx(
+                        out=acc[:],
+                        lhsT=y_codes[:, g, l_cols].bitcast(FP8X4),
+                        lhsT_scale=y_scales[:, g, l_cols],
+                        rhs=w_codes[:, g, n_cols].bitcast(FP8X4),
+                        rhs_scale=w_scales[:, g, n_cols],
+                        start=(g == 0),
+                        stop=(g == PASSES - 1),
+                    )
+                result = results.tile([P, N_CHUNK], F32)
+                nc.vector.tensor_tensor(out=result[:], in0=acc[:], in1=bias[:, n_cols], op=ALU.add)
+                nc.sync.dma_start(out=out_rows[l_cols, n_cols], in_=result[:])
+
+        def prepare_y(j):
+            for g in range(PASSES):
+                quantise_y(j, g)
+
+        def prepare_w(c):
+            for g in range(PASSES):
+                quantise_w(c, g)
+
+        norms(0)
+        prepare_y(0)
+        norms(1)
+        prepare_w(0)
+        multiply(0, 0)
+        prepare_y(1)
+        multiply(1, 0)
+        norms(2)
+        prepare_w(1)
+        multiply(0, 1)
+        multiply(1, 1)
+        prepare_y(2)
+        multiply(2, 0)
+        multiply(2, 1)
+        norms(3)
+        prepare_y(3)
+        multiply(3, 0)
+        multiply(3, 1)
+        for c in range(2, CHUNKS):
+            prepare_w(c)
+            for j in range(GROUPS):
+                multiply(j, c)

@@ -163,7 +163,7 @@ def tile_normlocalattention_pb_kernel(tc, o_attn, Wo, bo, norm_scale, norm_gate,
                         op1=ALU.mult,
                     )
             y_bf = work.tile([P, L_GROUP, PACK], BF16, align_bytes=64)
-            nc.vector.tensor_tensor(
+            nc.gpsimd.tensor_tensor(
                 out=y_bf[:],
                 in0=scaled[:].rearrange("p t l -> p l t"),
                 in1=inv_r[:, cols].unsqueeze(2).to_broadcast([P, L_GROUP, PACK]),

@@ -34,6 +34,11 @@ N_LOAD = 256
 N_TILES = N_LOAD // P
 LOADS_PER_CHUNK = N_CHUNK // N_LOAD
 
+SLOTS = GROUPS * PASSES
+PIECES = PASSES
+PIECE_K = L_TILES * K // PIECES
+TILES_PER_SLOT = 2
+
 FLOPS = 2 * L * K * N
 
 
@@ -43,11 +48,15 @@ def tile_normlocalattention_pb_kernel(tc, o_attn, Wo, bo, norm_scale, norm_gate,
     out_rows = out.flatten_outer_dims()
 
     with ExitStack() as stack:
+        stack.enter_context(tc.manual_schedule())
         keep = stack.enter_context(tc.tile_pool(name="keep", bufs=1))
-        work = stack.enter_context(tc.tile_pool(name="work", bufs=2))
+        small = stack.enter_context(tc.tile_pool(name="small", bufs=2))
+        three = stack.enter_context(tc.tile_pool(name="three", bufs=3))
+        two = stack.enter_context(tc.tile_pool(name="two", bufs=2))
         results = stack.enter_context(tc.tile_pool(name="results", bufs=4))
-        flipped = stack.enter_context(tc.psum_pool(name="flipped", bufs=5))
-        sums = stack.enter_context(tc.psum_pool(name="sums", bufs=3))
+        y_banks = stack.enter_context(tc.psum_pool(name="y_banks", bufs=2))
+        w_banks = stack.enter_context(tc.psum_pool(name="w_banks", bufs=2))
+        sums = stack.enter_context(tc.psum_pool(name="sums", bufs=4))
 
         ident = keep.tile([P, P], F32)
         make_identity(nc, ident[:])
@@ -74,21 +83,19 @@ def tile_normlocalattention_pb_kernel(tc, o_attn, Wo, bo, norm_scale, norm_gate,
                 nc.sync.dma_start(out=w_sb[h][:], in_=rows.rearrange("(i p) k -> p i k", p=P))
 
         load_o(0)
-        load_w(0)
         load_o(1)
-        nc.sync.dma_start(out=bias[:], in_=bo.partition_broadcast(P))
+        load_w(0)
         load_w(1)
+        nc.sync.dma_start(out=bias[:], in_=bo.partition_broadcast(P))
         load_o(2)
-        load_o(3)
         load_w(2)
+        load_o(3)
         load_w(3)
 
-        vec_t = flipped.tile([P, HALVES, N_LOAD], F32, tag="flip")
-        nc.tensor.transpose(vec_t[:, 0, 0:P], vec_rows[:].bitcast(F32), ident[:])
+        vec_t = sums.tile([P, N_CHUNK], F32, tag="sum")
+        nc.tensor.transpose(vec_t[:, 0:P], vec_rows[:].bitcast(F32), ident[:])
         per_channel = keep.tile([P, 2 * BLOCKS * PAIR], F32)
-        nc.vector.tensor_copy(
-            out=per_channel[:], in_=vec_t[:, 0, 0 : 2 * BLOCKS].bitcast(BF16)
-        )
+        nc.vector.tensor_copy(out=per_channel[:], in_=vec_t[:, 0 : 2 * BLOCKS].bitcast(BF16))
 
         def gate_of(b, e):
             col = b * PAIR + e
@@ -103,9 +110,13 @@ def tile_normlocalattention_pb_kernel(tc, o_attn, Wo, bo, norm_scale, norm_gate,
         w_codes = keep.tile([P, PASSES, N], U32, align_bytes=64)
         w_scales = keep.tile([P, PASSES, N], U8, align_bytes=64)
         inv_r = keep.tile([P, L], F32)
+        sum_sq = [keep.tile([P, L_TILES, PIECES // L_TILES], F32, name="sum_sq%d" % j) for j in range(GROUPS)]
 
-        def flip_words(rows_sb, g):
-            bank = flipped.tile([P, HALVES, N_LOAD], F32, tag="flip")
+        y_bank, gated_of, scaled_of, y_bf_of = {}, {}, {}, {}
+        w_bank, w_bf_of = {}, {}
+        repeated_of, spread_of, sum_of = {}, {}, {}
+
+        def flip_words(bank, rows_sb, g):
             for u in range(HALVES):
                 b = g * HALVES + u
                 for i in range(N_TILES):
@@ -114,128 +125,199 @@ def tile_normlocalattention_pb_kernel(tc, o_attn, Wo, bo, norm_scale, norm_gate,
                         rows_sb[:, i, :].bitcast(F32)[:, b * P : (b + 1) * P],
                         ident[:],
                     )
-            return bank
+
+        def squares(j, q):
+            i, part = divmod(q, PIECES // L_TILES)
+            junk = two.tile([P, PIECE_K], BF16)
+            nc.scalar.activation(
+                out=junk[:],
+                in_=o_sb[j][:, i, part * PIECE_K : (part + 1) * PIECE_K],
+                func=ACT.Square,
+                accum_out=sum_sq[j][:, i, part : part + 1],
+            )
 
         def norms(j):
-            sum_sq = work.tile([P, L_TILES], F32)
-            for i in range(L_TILES):
-                squares = work.tile([P, K], BF16)
-                nc.scalar.activation(
-                    out=squares[:], in_=o_sb[j][:, i, :], func=ACT.Square, accum_out=sum_sq[:, i : i + 1]
-                )
-            root = work.tile([P, L_TILES], F32)
-            nc.gpsimd.tensor_tensor(out=root[:], in0=sum_sq[:], in1=half[:], op=ALU.pow)
-            r_eps = work.tile([P, L_TILES], F32)
+            total = small.tile([P, L_TILES], F32)
+            nc.gpsimd.tensor_tensor(out=total[:], in0=sum_sq[j][:, :, 0], in1=sum_sq[j][:, :, 1], op=ALU.add)
+            root = small.tile([P, L_TILES], F32)
+            nc.gpsimd.tensor_tensor(out=root[:], in0=total[:], in1=half[:], op=ALU.pow)
+            r_eps = small.tile([P, L_TILES], F32)
             nc.vector.tensor_scalar(
                 out=r_eps[:], in0=root[:], scalar1=K**-0.5, scalar2=EPS, op0=ALU.mult, op1=ALU.add
             )
-            inv = work.tile([P, L_TILES], F32)
+            inv = small.tile([P, L_TILES], F32)
             nc.vector.reciprocal(out=inv[:], in_=r_eps[:])
-            repeated = work.tile([P, L_TILES, P], F32)
+            repeated = small.tile([P, L_TILES, P], F32)
             nc.vector.tensor_copy(out=repeated[:], in_=inv[:].unsqueeze(2).to_broadcast([P, L_TILES, P]))
-            spread = flipped.tile([P, HALVES, N_LOAD], F32, tag="flip")
-            for i in range(L_TILES):
-                nc.tensor.transpose(spread[:, 0, i * P : (i + 1) * P], repeated[:, i, :], ident[:])
-            nc.vector.tensor_copy(out=inv_r[:, j * L_GROUP : (j + 1) * L_GROUP], in_=spread[:, 0, :])
+            repeated_of[j] = repeated
 
-        def quantise_y(j, g):
-            cols = slice(j * L_GROUP, (j + 1) * L_GROUP)
-            bank = flip_words(o_sb[j], g)
-            o_t = bank[:].bitcast(BF16).rearrange("p u (l e) -> p u l e", e=PAIR)
-            gated = work.tile([P, PACK, L_GROUP], F32)
+        def spread_norms(j):
+            spread = sums.tile([P, N_CHUNK], F32, tag="sum")
+            for i in range(L_TILES):
+                nc.tensor.transpose(spread[:, i * P : (i + 1) * P], repeated_of[j][:, i, :], ident[:])
+            spread_of[j] = spread
+
+        def keep_norms(j):
+            nc.vector.tensor_copy(out=inv_r[:, j * L_GROUP : (j + 1) * L_GROUP], in_=spread_of[j][:, 0:L_GROUP])
+
+        def flip_y(s):
+            j, g = divmod(s, PASSES)
+            bank = y_banks.tile([P, HALVES, L_GROUP], F32, tag="y")
+            flip_words(bank, o_sb[j], g)
+            y_bank[s] = bank
+
+        def o_t_of(s):
+            return y_bank[s][:].bitcast(BF16).rearrange("p u (l e) -> p u l e", e=PAIR)
+
+        def gate(s):
+            g = s % PASSES
+            gated = three.tile([P, PACK, L_GROUP], F32)
             for u in range(HALVES):
                 for e in range(PAIR):
                     nc.scalar.activation(
                         out=gated[:, u * PAIR + e, :],
-                        in_=o_t[:, u, :, e],
+                        in_=o_t_of(s)[:, u, :, e],
                         func=ACT.Sigmoid,
                         scale=gate_of(g * HALVES + u, e),
                     )
-            scaled = work.tile([P, PACK, L_GROUP], F32)
+            gated_of[s] = gated
+
+        def weigh(s):
+            g = s % PASSES
+            scaled = three.tile([P, PACK, L_GROUP], F32)
             for u in range(HALVES):
                 for e in range(PAIR):
                     nc.vector.scalar_tensor_tensor(
                         out=scaled[:, u * PAIR + e, :],
-                        in0=o_t[:, u, :, e],
+                        in0=o_t_of(s)[:, u, :, e],
                         scalar=scale_of(g * HALVES + u, e),
-                        in1=gated[:, u * PAIR + e, :],
+                        in1=gated_of[s][:, u * PAIR + e, :],
                         op0=ALU.mult,
                         op1=ALU.mult,
                     )
-            y_bf = work.tile([P, L_GROUP, PACK], BF16, align_bytes=64)
-            nc.gpsimd.tensor_tensor(
+            scaled_of[s] = scaled
+
+        def normalise(s):
+            j = s // PASSES
+            y_bf = two.tile([P, L_GROUP, PACK], BF16, align_bytes=64)
+            nc.vector.tensor_tensor(
                 out=y_bf[:],
-                in0=scaled[:].rearrange("p t l -> p l t"),
-                in1=inv_r[:, cols].unsqueeze(2).to_broadcast([P, L_GROUP, PACK]),
+                in0=scaled_of[s][:].rearrange("p t l -> p l t"),
+                in1=inv_r[:, j * L_GROUP : (j + 1) * L_GROUP].unsqueeze(2).to_broadcast([P, L_GROUP, PACK]),
                 op=ALU.mult,
             )
+            y_bf_of[s] = y_bf
+
+        def quantise_y(s):
+            j, g = divmod(s, PASSES)
+            cols = slice(j * L_GROUP, (j + 1) * L_GROUP)
             nc.vector.quantize_mx(
                 out=y_codes[:, g, cols].bitcast(FP8X4),
                 scales=y_scales[:, g, cols],
-                in_=y_bf[:].rearrange("p l t -> p (l t)"),
+                in_=y_bf_of[s][:].rearrange("p l t -> p (l t)"),
             )
 
-        def quantise_w(c, g):
-            cols = slice(c * N_CHUNK, (c + 1) * N_CHUNK)
-            w_bf = work.tile([P, N_CHUNK, PACK], BF16, align_bytes=64)
+        def flip_w(s):
+            c, g = divmod(s, PASSES)
             for h in range(LOADS_PER_CHUNK):
-                bank = flip_words(w_sb[c * LOADS_PER_CHUNK + h], g)
+                bank = w_banks.tile([P, HALVES, N_LOAD], F32, tag="w")
+                flip_words(bank, w_sb[c * LOADS_PER_CHUNK + h], g)
+                w_bank[(s, h)] = bank
+
+        def copy_w(s):
+            w_bf = three.tile([P, N_CHUNK, PACK], BF16, align_bytes=64)
+            for h in range(LOADS_PER_CHUNK):
                 nc.scalar.copy(
                     out=w_bf[:].bitcast(F32)[:, h * N_LOAD : (h + 1) * N_LOAD, :],
-                    in_=bank[:].rearrange("p u n -> p n u"),
+                    in_=w_bank[(s, h)][:].rearrange("p u n -> p n u"),
                 )
+            w_bf_of[s] = w_bf
+
+        def quantise_w(s):
+            c, g = divmod(s, PASSES)
+            cols = slice(c * N_CHUNK, (c + 1) * N_CHUNK)
             nc.vector.quantize_mx(
                 out=w_codes[:, g, cols].bitcast(FP8X4),
                 scales=w_scales[:, g, cols],
-                in_=w_bf[:].rearrange("p n t -> p (n t)"),
+                in_=w_bf_of[s][:].rearrange("p n t -> p (n t)"),
             )
 
-        def multiply(j, c):
+        def multiply(tile):
+            row_tile, c = tile
+            l_cols = slice(row_tile * P, (row_tile + 1) * P)
             n_cols = slice(c * N_CHUNK, (c + 1) * N_CHUNK)
-            for i in range(L_TILES):
-                l_cols = slice(j * L_GROUP + i * P, j * L_GROUP + (i + 1) * P)
-                acc = sums.tile([P, N_CHUNK], F32)
-                for g in range(PASSES):
-                    nc.tensor.matmul_mx(
-                        out=acc[:],
-                        lhsT=y_codes[:, g, l_cols].bitcast(FP8X4),
-                        lhsT_scale=y_scales[:, g, l_cols],
-                        rhs=w_codes[:, g, n_cols].bitcast(FP8X4),
-                        rhs_scale=w_scales[:, g, n_cols],
-                        start=(g == 0),
-                        stop=(g == PASSES - 1),
-                    )
-                result = results.tile([P, N_CHUNK], F32)
-                nc.vector.tensor_tensor(out=result[:], in0=acc[:], in1=bias[:, n_cols], op=ALU.add)
-                nc.sync.dma_start(out=out_rows[l_cols, n_cols], in_=result[:])
-
-        def prepare_y(j):
+            acc = sums.tile([P, N_CHUNK], F32, tag="sum")
             for g in range(PASSES):
-                quantise_y(j, g)
+                nc.tensor.matmul_mx(
+                    out=acc[:],
+                    lhsT=y_codes[:, g, l_cols].bitcast(FP8X4),
+                    lhsT_scale=y_scales[:, g, l_cols],
+                    rhs=w_codes[:, g, n_cols].bitcast(FP8X4),
+                    rhs_scale=w_scales[:, g, n_cols],
+                    start=(g == 0),
+                    stop=(g == PASSES - 1),
+                )
+            sum_of[tile] = acc
 
-        def prepare_w(c):
-            for g in range(PASSES):
-                quantise_w(c, g)
+        def add_bias(tile):
+            row_tile, c = tile
+            l_cols = slice(row_tile * P, (row_tile + 1) * P)
+            n_cols = slice(c * N_CHUNK, (c + 1) * N_CHUNK)
+            result = results.tile([P, N_CHUNK], F32)
+            nc.vector.tensor_tensor(out=result[:], in0=sum_of[tile][:], in1=bias[:, n_cols], op=ALU.add)
+            nc.sync.dma_start(out=out_rows[l_cols, n_cols], in_=result[:])
 
-        norms(0)
-        prepare_y(0)
-        norms(1)
-        prepare_w(0)
-        multiply(0, 0)
-        prepare_y(1)
-        multiply(1, 0)
-        norms(2)
-        prepare_w(1)
-        multiply(0, 1)
-        multiply(1, 1)
-        prepare_y(2)
-        multiply(2, 0)
-        multiply(2, 1)
-        norms(3)
-        prepare_y(3)
-        multiply(3, 0)
-        multiply(3, 1)
-        for c in range(2, CHUNKS):
-            prepare_w(c)
-            for j in range(GROUPS):
-                multiply(j, c)
+        def tiles_of(j, c):
+            return [(j * L_TILES + i, c) for i in range(L_TILES)]
+
+        for q in range(PIECES):
+            squares(0, q)
+        flip_y(0)
+
+        waiting = []
+        fresh = []
+        for s in range(SLOTS + 1):
+            j, g = divmod(s, PASSES)
+            before = s - 1
+
+            if g == 1:
+                spread_norms(j)
+            if s < SLOTS:
+                flip_w(s)
+            if s + 1 < SLOTS:
+                flip_y(s + 1)
+            now = waiting[:TILES_PER_SLOT]
+            waiting = waiting[TILES_PER_SLOT:] + fresh
+            fresh = []
+            for tile in now:
+                multiply(tile)
+
+            if s < SLOTS:
+                gate(s)
+                if j + 1 < GROUPS:
+                    squares(j + 1, g)
+                copy_w(s)
+
+            if g == 1:
+                keep_norms(j)
+            if s < SLOTS:
+                weigh(s)
+                if g == 0:
+                    norms(j)
+            if before >= 0:
+                quantise_w(before)
+                normalise(before)
+            for tile in now:
+                add_bias(tile)
+            if before >= 0:
+                quantise_y(before)
+                if before % PASSES == PASSES - 1:
+                    done = before // PASSES
+                    for other in range(done):
+                        fresh.extend(tiles_of(other, done))
+                    for c in range(done + 1):
+                        fresh.extend(tiles_of(done, c))
+
+        for tile in waiting + fresh:
+            multiply(tile)
+            add_bias(tile)

@@ -37,7 +37,8 @@ LOADS_PER_CHUNK = N_CHUNK // N_LOAD
 SLOTS = GROUPS * PASSES
 PIECES = PASSES
 PIECE_K = L_TILES * K // PIECES
-TILES_PER_SLOT = 2
+TILES_PER_SLOT = 3
+G_ROWS = 128
 
 FLOPS = 2 * L * K * N
 
@@ -52,7 +53,9 @@ def tile_normlocalattention_pb_kernel(tc, o_attn, Wo, bo, norm_scale, norm_gate,
         keep = stack.enter_context(tc.tile_pool(name="keep", bufs=1))
         small = stack.enter_context(tc.tile_pool(name="small", bufs=2))
         three = stack.enter_context(tc.tile_pool(name="three", bufs=3))
+        one = stack.enter_context(tc.tile_pool(name="one", bufs=1))
         two = stack.enter_context(tc.tile_pool(name="two", bufs=2))
+        four = stack.enter_context(tc.tile_pool(name="four", bufs=4))
         results = stack.enter_context(tc.tile_pool(name="results", bufs=4))
         y_banks = stack.enter_context(tc.psum_pool(name="y_banks", bufs=2))
         w_banks = stack.enter_context(tc.psum_pool(name="w_banks", bufs=2))
@@ -197,16 +200,22 @@ def tile_normlocalattention_pb_kernel(tc, o_attn, Wo, bo, norm_scale, norm_gate,
                     )
             scaled_of[s] = scaled
 
-        def normalise(s):
-            j = s // PASSES
-            y_bf = two.tile([P, L_GROUP, PACK], BF16, align_bytes=64)
-            nc.vector.tensor_tensor(
-                out=y_bf[:],
-                in0=scaled_of[s][:].rearrange("p t l -> p l t"),
-                in1=inv_r[:, j * L_GROUP : (j + 1) * L_GROUP].unsqueeze(2).to_broadcast([P, L_GROUP, PACK]),
+        def normalise(engine, s, first, rows):
+            start = (s // PASSES) * L_GROUP + first
+            engine.tensor_tensor(
+                out=y_bf_of[s][:, first : first + rows, :],
+                in0=scaled_of[s][:, :, first : first + rows].rearrange("p t l -> p l t"),
+                in1=inv_r[:, start : start + rows].unsqueeze(2).to_broadcast([P, rows, PACK]),
                 op=ALU.mult,
             )
+
+        def normalise_on_gpsimd(s):
+            y_bf = one.tile([P, L_GROUP, PACK], BF16, align_bytes=64)
             y_bf_of[s] = y_bf
+            normalise(nc.gpsimd, s, 0, G_ROWS)
+
+        def normalise_on_vector(s):
+            normalise(nc.vector, s, G_ROWS, L_GROUP - G_ROWS)
 
         def quantise_y(s):
             j, g = divmod(s, PASSES)
@@ -225,7 +234,7 @@ def tile_normlocalattention_pb_kernel(tc, o_attn, Wo, bo, norm_scale, norm_gate,
                 w_bank[(s, h)] = bank
 
         def copy_w(s):
-            w_bf = three.tile([P, N_CHUNK, PACK], BF16, align_bytes=64)
+            w_bf = four.tile([P, N_CHUNK, PACK], BF16, align_bytes=64)
             for h in range(LOADS_PER_CHUNK):
                 nc.scalar.copy(
                     out=w_bf[:].bitcast(F32)[:, h * N_LOAD : (h + 1) * N_LOAD, :],
@@ -267,28 +276,34 @@ def tile_normlocalattention_pb_kernel(tc, o_attn, Wo, bo, norm_scale, norm_gate,
             nc.vector.tensor_tensor(out=result[:], in0=sum_of[tile][:], in1=bias[:, n_cols], op=ALU.add)
             nc.sync.dma_start(out=out_rows[l_cols, n_cols], in_=result[:])
 
+        def w_units_of(s):
+            last = SLOTS - PASSES
+            if s < last:
+                return [s]
+            return [w for w in (last + 2 * (s - last), last + 2 * (s - last) + 1) if w < SLOTS]
+
         def tiles_of(j, c):
             return [(j * L_TILES + i, c) for i in range(L_TILES)]
 
         for q in range(PIECES):
             squares(0, q)
+        norms(0)
         flip_y(0)
 
         waiting = []
-        fresh = []
+        groups_done, chunks_done = [], []
         for s in range(SLOTS + 1):
             j, g = divmod(s, PASSES)
             before = s - 1
 
-            if g == 1:
-                spread_norms(j)
-            if s < SLOTS:
-                flip_w(s)
+            for w in w_units_of(s)[:1]:
+                flip_w(w)
             if s + 1 < SLOTS:
                 flip_y(s + 1)
+            if g == 0 and s < SLOTS:
+                spread_norms(j)
             now = waiting[:TILES_PER_SLOT]
-            waiting = waiting[TILES_PER_SLOT:] + fresh
-            fresh = []
+            waiting = waiting[TILES_PER_SLOT:]
             for tile in now:
                 multiply(tile)
 
@@ -296,28 +311,36 @@ def tile_normlocalattention_pb_kernel(tc, o_attn, Wo, bo, norm_scale, norm_gate,
                 gate(s)
                 if j + 1 < GROUPS:
                     squares(j + 1, g)
-                copy_w(s)
+            for w in w_units_of(s)[:1]:
+                copy_w(w)
+            for w in w_units_of(s)[1:]:
+                flip_w(w)
+                copy_w(w)
 
-            if g == 1:
-                keep_norms(j)
             if s < SLOTS:
                 weigh(s)
-                if g == 0:
-                    norms(j)
-            if before >= 0:
-                quantise_w(before)
-                normalise(before)
             for tile in now:
                 add_bias(tile)
+            if g == 0 and s < SLOTS:
+                keep_norms(j)
             if before >= 0:
+                normalise_on_vector(before)
+                for w in w_units_of(before):
+                    quantise_w(w)
+                    if w % PASSES == PASSES - 1:
+                        chunks_done.append(w // PASSES)
+                        for other in groups_done:
+                            waiting.extend(tiles_of(other, w // PASSES))
                 quantise_y(before)
                 if before % PASSES == PASSES - 1:
-                    done = before // PASSES
-                    for other in range(done):
-                        fresh.extend(tiles_of(other, done))
-                    for c in range(done + 1):
-                        fresh.extend(tiles_of(done, c))
+                    groups_done.append(before // PASSES)
+                    for c in chunks_done:
+                        waiting.extend(tiles_of(before // PASSES, c))
+            if g == PASSES - 1 and j + 1 < GROUPS:
+                norms(j + 1)
+            if s < SLOTS:
+                normalise_on_gpsimd(s)
 
-        for tile in waiting + fresh:
+        for tile in waiting:
             multiply(tile)
             add_bias(tile)

@@ -55,7 +55,6 @@ def tile_normlocalattention_pb_kernel(tc, o_attn, Wo, bo, norm_scale, norm_gate,
         three = stack.enter_context(tc.tile_pool(name="three", bufs=3))
         one = stack.enter_context(tc.tile_pool(name="one", bufs=1))
         two = stack.enter_context(tc.tile_pool(name="two", bufs=2))
-        four = stack.enter_context(tc.tile_pool(name="four", bufs=4))
         results = stack.enter_context(tc.tile_pool(name="results", bufs=4))
         y_banks = stack.enter_context(tc.psum_pool(name="y_banks", bufs=2))
         w_banks = stack.enter_context(tc.psum_pool(name="w_banks", bufs=2))
@@ -233,14 +232,19 @@ def tile_normlocalattention_pb_kernel(tc, o_attn, Wo, bo, norm_scale, norm_gate,
                 flip_words(bank, w_sb[c * LOADS_PER_CHUNK + h], g)
                 w_bank[(s, h)] = bank
 
-        def copy_w(s):
-            w_bf = four.tile([P, N_CHUNK, PACK], BF16, align_bytes=64)
-            for h in range(LOADS_PER_CHUNK):
-                nc.scalar.copy(
-                    out=w_bf[:].bitcast(F32)[:, h * N_LOAD : (h + 1) * N_LOAD, :],
-                    in_=w_bank[(s, h)][:].rearrange("p u n -> p n u"),
-                )
+        def copy_w(copy, s, h):
+            copy(
+                out=w_bf_of[s][:].bitcast(F32)[:, h * N_LOAD : (h + 1) * N_LOAD, :],
+                in_=w_bank[(s, h)][:].rearrange("p u n -> p n u"),
+            )
+
+        def copy_w_on_scalar(s):
+            w_bf = three.tile([P, N_CHUNK, PACK], BF16, align_bytes=64)
             w_bf_of[s] = w_bf
+            copy_w(nc.scalar.copy, s, 0)
+
+        def copy_w_on_vector(s):
+            copy_w(nc.vector.tensor_copy, s, 1)
 
         def quantise_w(s):
             c, g = divmod(s, PASSES)
@@ -276,12 +280,6 @@ def tile_normlocalattention_pb_kernel(tc, o_attn, Wo, bo, norm_scale, norm_gate,
             nc.vector.tensor_tensor(out=result[:], in0=sum_of[tile][:], in1=bias[:, n_cols], op=ALU.add)
             nc.sync.dma_start(out=out_rows[l_cols, n_cols], in_=result[:])
 
-        def w_units_of(s):
-            last = SLOTS - PASSES
-            if s < last:
-                return [s]
-            return [w for w in (last + 2 * (s - last), last + 2 * (s - last) + 1) if w < SLOTS]
-
         def tiles_of(j, c):
             return [(j * L_TILES + i, c) for i in range(L_TILES)]
 
@@ -296,8 +294,8 @@ def tile_normlocalattention_pb_kernel(tc, o_attn, Wo, bo, norm_scale, norm_gate,
             j, g = divmod(s, PASSES)
             before = s - 1
 
-            for w in w_units_of(s)[:1]:
-                flip_w(w)
+            if s < SLOTS:
+                flip_w(s)
             if s + 1 < SLOTS:
                 flip_y(s + 1)
             if g == 0 and s < SLOTS:
@@ -311,26 +309,22 @@ def tile_normlocalattention_pb_kernel(tc, o_attn, Wo, bo, norm_scale, norm_gate,
                 gate(s)
                 if j + 1 < GROUPS:
                     squares(j + 1, g)
-            for w in w_units_of(s)[:1]:
-                copy_w(w)
-            for w in w_units_of(s)[1:]:
-                flip_w(w)
-                copy_w(w)
+                copy_w_on_scalar(s)
 
             if s < SLOTS:
                 weigh(s)
+                copy_w_on_vector(s)
             for tile in now:
                 add_bias(tile)
             if g == 0 and s < SLOTS:
                 keep_norms(j)
             if before >= 0:
                 normalise_on_vector(before)
-                for w in w_units_of(before):
-                    quantise_w(w)
-                    if w % PASSES == PASSES - 1:
-                        chunks_done.append(w // PASSES)
-                        for other in groups_done:
-                            waiting.extend(tiles_of(other, w // PASSES))
+                quantise_w(before)
+                if before % PASSES == PASSES - 1:
+                    chunks_done.append(before // PASSES)
+                    for other in groups_done:
+                        waiting.extend(tiles_of(other, before // PASSES))
                 quantise_y(before)
                 if before % PASSES == PASSES - 1:
                     groups_done.append(before // PASSES)

from contextlib import ExitStack

import concourse.mybir as mybir
from concourse.masks import make_identity

F32 = mybir.dt.float32
BF16 = mybir.dt.bfloat16
U32 = mybir.dt.uint32
U8 = mybir.dt.uint8
FP8X4 = mybir.dt.float8_e4m3fn_x4
ACT = mybir.ActivationFunctionType
ALU = mybir.AluOpType

P = 128
L = 1024
K = 2048
N = 2048
EPS = 1e-8

PACK = 4
K_PASS = P * PACK
PASSES = K // K_PASS
PAIR = 2
HALVES = PACK // PAIR
BLOCK_K = P * PAIR
BLOCKS = K // BLOCK_K

L_GROUP = 256
L_TILES = L_GROUP // P
GROUPS = L // L_GROUP
N_CHUNK = 512
CHUNKS = N // N_CHUNK
N_LOAD = 256
N_TILES = N_LOAD // P
LOADS_PER_CHUNK = N_CHUNK // N_LOAD

SLOTS = GROUPS * PASSES
PIECES = PASSES
PIECE_K = L_TILES * K // PIECES
TILES_PER_SLOT = 3
G_ROWS = 128

FLOPS = 2 * L * K * N


def tile_normlocalattention_pb_kernel(tc, o_attn, Wo, bo, norm_scale, norm_gate, out):
    nc = tc.nc
    o_rows = o_attn.flatten_outer_dims()
    out_rows = out.flatten_outer_dims()

    with ExitStack() as stack:
        stack.enter_context(tc.manual_schedule())
        keep = stack.enter_context(tc.tile_pool(name="keep", bufs=1))
        small = stack.enter_context(tc.tile_pool(name="small", bufs=2))
        three = stack.enter_context(tc.tile_pool(name="three", bufs=3))
        one = stack.enter_context(tc.tile_pool(name="one", bufs=1))
        two = stack.enter_context(tc.tile_pool(name="two", bufs=2))
        results = stack.enter_context(tc.tile_pool(name="results", bufs=4))
        y_banks = stack.enter_context(tc.psum_pool(name="y_banks", bufs=2))
        w_banks = stack.enter_context(tc.psum_pool(name="w_banks", bufs=2))
        sums = stack.enter_context(tc.psum_pool(name="sums", bufs=4))

        ident = keep.tile([P, P], F32)
        make_identity(nc, ident[:])
        half = keep.tile([P, L_TILES], F32)
        nc.vector.memset(half[:], 0.5)
        vec_rows = keep.tile([P, BLOCK_K], BF16)
        nc.vector.memset(vec_rows[:], 0.0)

        nc.sync.dma_start(out=vec_rows[0:BLOCKS, :], in_=norm_gate.rearrange("(b c) -> b c", c=BLOCK_K))
        nc.sync.dma_start(
            out=vec_rows[BLOCKS : 2 * BLOCKS, :], in_=norm_scale.rearrange("(b c) -> b c", c=BLOCK_K)
        )
        o_sb = [keep.tile([P, L_TILES, K], BF16, name="o_sb%d" % j) for j in range(GROUPS)]
        w_sb = [keep.tile([P, N_TILES, K], BF16, name="w_sb%d" % h) for h in range(N // N_LOAD)]
        bias = keep.tile([P, N], BF16)

        def load_o(j):
            rows = o_rows[j * L_GROUP : (j + 1) * L_GROUP, :]
            nc.sync.dma_start(out=o_sb[j][:], in_=rows.rearrange("(i p) k -> p i k", p=P))

        def load_w(c):
            for h in range(c * LOADS_PER_CHUNK, (c + 1) * LOADS_PER_CHUNK):
                rows = Wo[h * N_LOAD : (h + 1) * N_LOAD, :]
                nc.sync.dma_start(out=w_sb[h][:], in_=rows.rearrange("(i p) k -> p i k", p=P))

        load_o(0)
        load_o(1)
        load_w(0)
        load_w(1)
        nc.sync.dma_start(out=bias[:], in_=bo.partition_broadcast(P))
        load_o(2)
        load_w(2)
        load_o(3)
        load_w(3)

        vec_t = sums.tile([P, N_CHUNK], F32, tag="sum")
        nc.tensor.transpose(vec_t[:, 0:P], vec_rows[:].bitcast(F32), ident[:])
        per_channel = keep.tile([P, 2 * BLOCKS * PAIR], F32)
        nc.vector.tensor_copy(out=per_channel[:], in_=vec_t[:, 0 : 2 * BLOCKS].bitcast(BF16))

        def gate_of(b, e):
            col = b * PAIR + e
            return per_channel[:, col : col + 1]

        def scale_of(b, e):
            col = (BLOCKS + b) * PAIR + e
            return per_channel[:, col : col + 1]

        y_codes = keep.tile([P, PASSES, L], U32, align_bytes=64)
        y_scales = keep.tile([P, PASSES, L], U8, align_bytes=64)
        w_codes = keep.tile([P, PASSES, N], U32, align_bytes=64)
        w_scales = keep.tile([P, PASSES, N], U8, align_bytes=64)
        inv_r = keep.tile([P, L], F32)
        sum_sq = [keep.tile([P, L_TILES, PIECES // L_TILES], F32, name="sum_sq%d" % j) for j in range(GROUPS)]

        y_bank, gated_of, scaled_of, y_bf_of = {}, {}, {}, {}
        w_bank, w_bf_of = {}, {}
        repeated_of, spread_of, sum_of = {}, {}, {}

        def flip_words(bank, rows_sb, g):
            for u in range(HALVES):
                b = g * HALVES + u
                for i in range(N_TILES):
                    nc.tensor.transpose(
                        bank[:, u, i * P : (i + 1) * P],
                        rows_sb[:, i, :].bitcast(F32)[:, b * P : (b + 1) * P],
                        ident[:],
                    )

        def squares(j, q):
            i, part = divmod(q, PIECES // L_TILES)
            junk = two.tile([P, PIECE_K], BF16)
            nc.scalar.activation(
                out=junk[:],
                in_=o_sb[j][:, i, part * PIECE_K : (part + 1) * PIECE_K],
                func=ACT.Square,
                accum_out=sum_sq[j][:, i, part : part + 1],
            )

        def norms(j):
            total = small.tile([P, L_TILES], F32)
            nc.gpsimd.tensor_tensor(out=total[:], in0=sum_sq[j][:, :, 0], in1=sum_sq[j][:, :, 1], op=ALU.add)
            root = small.tile([P, L_TILES], F32)
            nc.gpsimd.tensor_tensor(out=root[:], in0=total[:], in1=half[:], op=ALU.pow)
            r_eps = small.tile([P, L_TILES], F32)
            nc.vector.tensor_scalar(
                out=r_eps[:], in0=root[:], scalar1=K**-0.5, scalar2=EPS, op0=ALU.mult, op1=ALU.add
            )
            inv = small.tile([P, L_TILES], F32)
            nc.vector.reciprocal(out=inv[:], in_=r_eps[:])
            repeated = small.tile([P, L_TILES, P], F32)
            nc.vector.tensor_copy(out=repeated[:], in_=inv[:].unsqueeze(2).to_broadcast([P, L_TILES, P]))
            repeated_of[j] = repeated

        def spread_norms(j):
            spread = sums.tile([P, N_CHUNK], F32, tag="sum")
            for i in range(L_TILES):
                nc.tensor.transpose(spread[:, i * P : (i + 1) * P], repeated_of[j][:, i, :], ident[:])
            spread_of[j] = spread

        def keep_norms(j):
            nc.vector.tensor_copy(out=inv_r[:, j * L_GROUP : (j + 1) * L_GROUP], in_=spread_of[j][:, 0:L_GROUP])

        def flip_y(s):
            j, g = divmod(s, PASSES)
            bank = y_banks.tile([P, HALVES, L_GROUP], F32, tag="y")
            flip_words(bank, o_sb[j], g)
            y_bank[s] = bank

        def o_t_of(s):
            return y_bank[s][:].bitcast(BF16).rearrange("p u (l e) -> p u l e", e=PAIR)

        def gate(s):
            g = s % PASSES
            gated = three.tile([P, PACK, L_GROUP], F32)
            for u in range(HALVES):
                for e in range(PAIR):
                    nc.scalar.activation(
                        out=gated[:, u * PAIR + e, :],
                        in_=o_t_of(s)[:, u, :, e],
                        func=ACT.Sigmoid,
                        scale=gate_of(g * HALVES + u, e),
                    )
            gated_of[s] = gated

        def weigh(s):
            g = s % PASSES
            scaled = three.tile([P, PACK, L_GROUP], F32)
            for u in range(HALVES):
                for e in range(PAIR):
                    nc.vector.scalar_tensor_tensor(
                        out=scaled[:, u * PAIR + e, :],
                        in0=o_t_of(s)[:, u, :, e],
                        scalar=scale_of(g * HALVES + u, e),
                        in1=gated_of[s][:, u * PAIR + e, :],
                        op0=ALU.mult,
                        op1=ALU.mult,
                    )
            scaled_of[s] = scaled

        def normalise(engine, s, first, rows):
            start = (s // PASSES) * L_GROUP + first
            engine.tensor_tensor(
                out=y_bf_of[s][:, first : first + rows, :],
                in0=scaled_of[s][:, :, first : first + rows].rearrange("p t l -> p l t"),
                in1=inv_r[:, start : start + rows].unsqueeze(2).to_broadcast([P, rows, PACK]),
                op=ALU.mult,
            )

        def normalise_on_gpsimd(s):
            y_bf = one.tile([P, L_GROUP, PACK], BF16, align_bytes=64)
            y_bf_of[s] = y_bf
            normalise(nc.gpsimd, s, 0, G_ROWS)

        def normalise_on_vector(s):
            normalise(nc.vector, s, G_ROWS, L_GROUP - G_ROWS)

        def quantise_y(s):
            j, g = divmod(s, PASSES)
            cols = slice(j * L_GROUP, (j + 1) * L_GROUP)
            nc.vector.quantize_mx(
                out=y_codes[:, g, cols].bitcast(FP8X4),
                scales=y_scales[:, g, cols],
                in_=y_bf_of[s][:].rearrange("p l t -> p (l t)"),
            )

        def flip_w(s):
            c, g = divmod(s, PASSES)
            for h in range(LOADS_PER_CHUNK):
                bank = w_banks.tile([P, HALVES, N_LOAD], F32, tag="w")
                flip_words(bank, w_sb[c * LOADS_PER_CHUNK + h], g)
                w_bank[(s, h)] = bank

        def copy_w(copy, s, h):
            copy(
                out=w_bf_of[s][:].bitcast(F32)[:, h * N_LOAD : (h + 1) * N_LOAD, :],
                in_=w_bank[(s, h)][:].rearrange("p u n -> p n u"),
            )

        def copy_w_on_scalar(s):
            w_bf = three.tile([P, N_CHUNK, PACK], BF16, align_bytes=64)
            w_bf_of[s] = w_bf
            copy_w(nc.scalar.copy, s, 0)

        def copy_w_on_vector(s):
            copy_w(nc.vector.tensor_copy, s, 1)

        def quantise_w(s):
            c, g = divmod(s, PASSES)
            cols = slice(c * N_CHUNK, (c + 1) * N_CHUNK)
            nc.vector.quantize_mx(
                out=w_codes[:, g, cols].bitcast(FP8X4),
                scales=w_scales[:, g, cols],
                in_=w_bf_of[s][:].rearrange("p n t -> p (n t)"),
            )

        def multiply(tile):
            row_tile, c = tile
            l_cols = slice(row_tile * P, (row_tile + 1) * P)
            n_cols = slice(c * N_CHUNK, (c + 1) * N_CHUNK)
            acc = sums.tile([P, N_CHUNK], F32, tag="sum")
            for g in range(PASSES):
                nc.tensor.matmul_mx(
                    out=acc[:],
                    lhsT=y_codes[:, g, l_cols].bitcast(FP8X4),
                    lhsT_scale=y_scales[:, g, l_cols],
                    rhs=w_codes[:, g, n_cols].bitcast(FP8X4),
                    rhs_scale=w_scales[:, g, n_cols],
                    start=(g == 0),
                    stop=(g == PASSES - 1),
                )
            sum_of[tile] = acc

        def add_bias(tile):
            row_tile, c = tile
            l_cols = slice(row_tile * P, (row_tile + 1) * P)
            n_cols = slice(c * N_CHUNK, (c + 1) * N_CHUNK)
            result = results.tile([P, N_CHUNK], F32)
            nc.vector.tensor_tensor(out=result[:], in0=sum_of[tile][:], in1=bias[:, n_cols], op=ALU.add)
            nc.sync.dma_start(out=out_rows[l_cols, n_cols], in_=result[:])

        def tiles_of(j, c):
            return [(j * L_TILES + i, c) for i in range(L_TILES)]

        for q in range(PIECES):
            squares(0, q)
        norms(0)
        flip_y(0)

        waiting = []
        groups_done, chunks_done = [], []
        for s in range(SLOTS + 1):
            j, g = divmod(s, PASSES)
            before = s - 1

            if s < SLOTS:
                flip_w(s)
            if s + 1 < SLOTS:
                flip_y(s + 1)
            if g == 0 and s < SLOTS:
                spread_norms(j)
            now = waiting[:TILES_PER_SLOT]
            waiting = waiting[TILES_PER_SLOT:]
            for tile in now:
                multiply(tile)

            if s < SLOTS:
                gate(s)
                if j + 1 < GROUPS:
                    squares(j + 1, g)
                copy_w_on_scalar(s)

            if s < SLOTS:
                weigh(s)
                copy_w_on_vector(s)
            for tile in now:
                add_bias(tile)
            if g == 0 and s < SLOTS:
                keep_norms(j)
            if before >= 0:
                normalise_on_vector(before)
                quantise_w(before)
                if before % PASSES == PASSES - 1:
                    chunks_done.append(before // PASSES)
                    for other in groups_done:
                        waiting.extend(tiles_of(other, before // PASSES))
                quantise_y(before)
                if before % PASSES == PASSES - 1:
                    groups_done.append(before // PASSES)
                    for c in chunks_done:
                        waiting.extend(tiles_of(before // PASSES, c))
            if g == PASSES - 1 and j + 1 < GROUPS:
                norms(j + 1)
            if s < SLOTS:
                normalise_on_gpsimd(s)

        for tile in waiting:
            multiply(tile)
            add_bias(tile)
